import numpy as np
import ml_dtypes


BF16 = ml_dtypes.bfloat16


def bf(x):
    return np.asarray(x, np.float32).astype(BF16)


def f64(x):
    return np.asarray(x).astype(np.float64)


E2M1 = np.array([0.0, 0.5, 1.0, 1.5, 2.0, 3.0, 4.0, 6.0, -0.0, -0.5, -1.0, -1.5, -2.0, -3.0, -4.0, -6.0])


def pack_weight(w, fmt):
    k, n = w.shape
    w = f64(bf(w)).reshape(k // 32, 32, n)
    amax = np.abs(w).max(1)
    if fmt == "e4m3":
        byte = np.frexp(amax)[1] - 1 + 127 - 7
    else:
        mant, ex = np.frexp(amax / 6.0)
        byte = np.where(mant > 0.5, ex, ex - 1) + 127
    byte = np.clip(np.where(amax > 0, byte, 1), 1, 254)
    scaled = (w * np.exp2(127.0 - byte)[:, None, :]).reshape(k, n).astype(np.float32)
    by_word = np.ascontiguousarray(scaled.reshape(k // 512, 128, 4, n).transpose(0, 1, 3, 2))
    if fmt == "e4m3":
        words = by_word.astype(ml_dtypes.float8_e4m3fn).view(np.uint8)
    else:
        c = by_word.astype(ml_dtypes.float4_e2m1fn).view(np.uint8) & 0xF
        words = c[..., 0::2] | (c[..., 1::2] << 4)
    return np.ascontiguousarray(words), np.ascontiguousarray(byte.astype(np.uint8).reshape(k // 512, 16, n))


def unpack_weight(words, scales, fmt):
    g, p, n, _ = words.shape
    if fmt == "e4m3":
        vals = np.ascontiguousarray(words).view(ml_dtypes.float8_e4m3fn).astype(np.float64)
    else:
        nib = np.empty((g, p, n, 4), np.uint8)
        nib[..., 0::2] = words & 0xF
        nib[..., 1::2] = words >> 4
        vals = E2M1[nib]
    vals = vals * np.repeat(np.exp2(scales.astype(np.float64) - 127.0), 8, axis=1)[..., None]
    return vals.transpose(0, 1, 3, 2).reshape(g * 512, n)

def pack4(w):
    words, scales = pack_weight(w, "e2m1")
    return words.reshape(words.shape[0], 128, -1), scales


def unpack4(words, scales):
    return unpack_weight(words.reshape(words.shape[0], 128, -1, 2), scales, "e2m1")


def kspread(k):
    return np.exp2(np.repeat(np.random.randint(-6, 7, k // 32), 32).astype(np.float64))


N, C, H = 512, 4096, 16
D = C // H
SIN_TIME = 10000.0


def create_sinusoidal_positions(n_pos, dim, time):
    denom = np.power(time, 2 * (np.arange(dim) // 2) / dim)
    position_enc = np.arange(n_pos)[:, None] / denom[None, :]
    return np.concatenate([np.sin(position_enc[:, 0::2]), np.cos(position_enc[:, 1::2])], axis=-1)


def apply_rope(x, time):
    pos = create_sinusoidal_positions(x.shape[-2], x.shape[-1], time)
    sin, cos = np.split(pos, 2, axis=-1)
    sin_pos = np.stack([sin, sin], axis=-1).reshape(pos.shape)
    cos_pos = np.stack([cos, cos], axis=-1).reshape(pos.shape)
    rotated = np.stack([-x[..., 1::2], x[..., ::2]], axis=-1).reshape(x.shape)
    return x * cos_pos + rotated * sin_pos


def setup_inputs():
    s = kspread(C)
    x = np.random.standard_normal((N, C)) * s
    x_words, x_scales = pack4(np.ascontiguousarray(x.T))
    w = np.random.standard_normal((2 * C, C)) / np.sqrt(C) / s[None, :]
    words, scales = pack4(np.ascontiguousarray(w.T))
    return {"x_words": x_words, "x_scales": x_scales, "W_qk_words": words, "W_qk_scales": scales}


def reference(x_words, x_scales, W_qk_words, W_qk_scales):
    qk = unpack4(x_words, x_scales).T @ unpack4(W_qk_words, W_qk_scales)
    qk = qk.reshape(N, 2, H, D).transpose(1, 2, 0, 3)
    q, k = qk[0], qk[1]
    return apply_rope(q, SIN_TIME), apply_rope(k, SIN_TIME)

@@ -1,0 +1,224 @@
+from contextlib import ExitStack
+import math
+
+import concourse.mybir as mybir
+
+F32 = mybir.dt.float32
+BF16 = mybir.dt.bfloat16
+I32 = mybir.dt.int32
+U8 = mybir.dt.uint8
+FP4X4 = mybir.dt.float4_e2m1fn_x4
+ALU = mybir.AluOpType
+ACT = mybir.ActivationFunctionType
+
+P = 128
+PASSES = 8
+TOK_TILES = 4
+BLOCK = 512
+BLOCKS = 16
+HEAD = 256
+PAIRS = 128
+RING = 6
+WARM = 18
+LAST_WIDTHS = [[512], [512], [256, 256], [256, 128, 128]]
+
+FLOPS = 2 * 512 * 4096 * 8192
+
+TWO_PI = 2.0 * math.pi
+TWO_PI_HI = 6.28125
+TWO_PI_LO = TWO_PI - TWO_PI_HI
+
+
+def tile_attentionblock_pa_kernel(tc, x_words, x_scales, W_qk_words, W_qk_scales, out_0, out_1):
+    nc = tc.nc
+    with ExitStack() as ctx:
+        keep = ctx.enter_context(tc.tile_pool(name="keep", bufs=1))
+        work = ctx.enter_context(tc.tile_pool(name="work", bufs=6))
+        outs = ctx.enter_context(tc.tile_pool(name="outs", bufs=8))
+        psum = ctx.enter_context(tc.psum_pool(name="psum", bufs=8))
+        ctx.enter_context(tc.manual_schedule())
+
+        x_codes = keep.tile([P, PASSES, 2 * 512], U8, name="x_codes", align_bytes=64)
+        x_planes = keep.tile([P, PASSES, 512], U8, name="x_planes", align_bytes=64)
+        w_codes = []
+        w_planes = []
+        for s in range(RING):
+            wc = keep.tile([P, PASSES, 2 * BLOCK], U8, name="w_codes%d" % s, align_bytes=64)
+            wp = keep.tile([P, PASSES, BLOCK], U8, name="w_planes%d" % s, align_bytes=64)
+            w_codes.append(wc)
+            w_planes.append(wp)
+
+        def load_codes(dst, words, g0, g1, c0, c1):
+            nc.sync.dma_start(
+                out=dst[:, g0:g1, :].bitcast(I32),
+                in_=words[g0:g1, :, c0:c1].rearrange("g p n -> p g n").bitcast(I32),
+            )
+
+        def load_scales(dst, scales, c0, c1):
+            for q in range(4):
+                nc.sync.dma_start(
+                    out=dst[32 * q : 32 * q + 4, :, :].bitcast(I32),
+                    in_=scales[:, 4 * q : 4 * q + 4, c0:c1].rearrange("g r n -> r g n").bitcast(I32),
+                )
+
+        def load_block(nb):
+            s = nb % RING
+            load_scales(w_planes[s], W_qk_scales, nb * BLOCK, (nb + 1) * BLOCK)
+            load_codes(w_codes[s], W_qk_words, 0, PASSES, nb * 2 * BLOCK, (nb + 1) * 2 * BLOCK)
+
+        warm_src = keep.tile([P, BLOCK], BF16, name="warm_src")
+        nc.vector.memset(warm_src[:], 1.0)
+        warm_acc = psum.tile([P, BLOCK], F32, name="acc", tag="acc")
+        for i in range(WARM):
+            nc.tensor.matmul(out=warm_acc[:], lhsT=warm_src[:, 0:P], rhs=warm_src[:], start=True, stop=True)
+        nc.gpsimd.memset(x_planes[:].bitcast(F32), 0.0)
+        nc.vector.memset(w_planes[0][:].bitcast(I32), 0)
+
+        pos_i = keep.tile([P, TOK_TILES], I32, name="pos_i")
+        nc.gpsimd.iota(pos_i[:], pattern=[[P, TOK_TILES]], base=0, channel_multiplier=1)
+        zero1 = keep.tile([P, 1], F32, name="zero1")
+        nc.gpsimd.memset(zero1[:], 0.0)
+        for s in range(1, RING):
+            nc.gpsimd.memset(w_planes[s][:].bitcast(F32), 0.0)
+
+        load_codes(x_codes, x_words, 0, 2, 0, 1024)
+        load_codes(w_codes[0], W_qk_words, 0, 2, 0, 1024)
+        load_scales(x_planes, x_scales, 0, 512)
+        load_scales(w_planes[0], W_qk_scales, 0, BLOCK)
+        load_codes(x_codes, x_words, 2, 5, 0, 1024)
+        load_codes(w_codes[0], W_qk_words, 2, 5, 0, 1024)
+        load_codes(x_codes, x_words, 5, 8, 0, 1024)
+        load_codes(w_codes[0], W_qk_words, 5, 8, 0, 1024)
+        for nb in range(1, RING):
+            load_block(nb)
+
+        warm = keep.tile([P, 1], F32, name="warm")
+        nc.scalar.activation(out=warm[:], in_=zero1[:], func=ACT.Sin)
+
+        W4 = TOK_TILES * PAIRS
+        pos_f = keep.tile([P, TOK_TILES], F32, name="pos_f")
+        nc.vector.tensor_copy(out=pos_f[:], in_=pos_i[:])
+        freq = keep.tile([P, PAIRS], F32, name="freq")
+        nc.vector.memset(freq[:, 0:1], 1.0)
+        for b in range(7):
+            w = 1 << b
+            nc.vector.tensor_scalar(
+                out=freq[:, w : 2 * w], in0=freq[:, 0:w], scalar1=10000.0 ** (-w / 128.0), scalar2=None, op0=ALU.mult
+            )
+        ang = keep.tile([P, W4], F32, name="ang")
+        for mt in range(TOK_TILES):
+            nc.vector.tensor_scalar(
+                out=ang[:, mt * PAIRS : (mt + 1) * PAIRS], in0=freq[:], scalar1=pos_f[:, mt : mt + 1], scalar2=None,
+                op0=ALU.mult,
+            )
+        turns_i = keep.tile([P, W4], I32, name="turns_i")
+        nc.vector.tensor_scalar(
+            out=turns_i[:], in0=ang[:], scalar1=1.0 / TWO_PI, scalar2=0.25, op0=ALU.mult, op1=ALU.add
+        )
+        turns = keep.tile([P, W4], F32, name="turns")
+        nc.vector.tensor_copy(out=turns[:], in_=turns_i[:])
+        red_hi = keep.tile([P, W4], F32, name="red_hi")
+        nc.vector.scalar_tensor_tensor(
+            out=red_hi[:], in0=turns[:], scalar=-TWO_PI_HI, in1=ang[:], op0=ALU.mult, op1=ALU.add
+        )
+        red = keep.tile([P, W4], F32, name="red")
+        nc.vector.scalar_tensor_tensor(
+            out=red[:], in0=turns[:], scalar=-TWO_PI_LO, in1=red_hi[:], op0=ALU.mult, op1=ALU.add
+        )
+        sin_half = keep.tile([P, W4], F32, name="sin_half")
+        nc.scalar.activation(out=sin_half[:], in_=red[:], func=ACT.Sin, scale=0.5)
+        neg_abs = keep.tile([P, W4], F32, name="neg_abs")
+        nc.vector.scalar_tensor_tensor(
+            out=neg_abs[:], in0=red[:], scalar=-1.0, in1=red[:], op0=ALU.mult, op1=ALU.min
+        )
+        co_arg = keep.tile([P, W4], F32, name="co_arg")
+        nc.vector.tensor_scalar(
+            out=co_arg[:], in0=neg_abs[:], scalar1=0.5, scalar2=0.5 * math.pi, op0=ALU.mult, op1=ALU.add
+        )
+        cos_half = keep.tile([P, W4], F32, name="cos_half")
+        nc.scalar.activation(out=cos_half[:], in_=co_arg[:], func=ACT.Sin)
+
+        sq = keep.tile([P, W4], F32, name="sq")
+        nc.vector.tensor_tensor(out=sq[:], in0=sin_half[:], in1=sin_half[:], op=ALU.mult)
+        cos_tab = keep.tile([P, W4, 2], F32, name="cos_tab")
+        nc.vector.tensor_scalar(
+            out=cos_tab[:], in0=sq[:].unsqueeze(2).to_broadcast([P, W4, 2]), scalar1=-2.0, scalar2=1.0,
+            op0=ALU.mult, op1=ALU.add,
+        )
+        sign2 = keep.tile([P, 2], F32, name="sign2")
+        nc.vector.memset(sign2[:, 0:1], -2.0)
+        nc.vector.memset(sign2[:, 1:2], 2.0)
+        sc = keep.tile([P, W4], F32, name="sc")
+        nc.vector.tensor_tensor(out=sc[:], in0=sin_half[:], in1=cos_half[:], op=ALU.mult)
+        sin_tab = keep.tile([P, W4, 2], F32, name="sin_tab")
+        nc.vector.tensor_tensor(
+            out=sin_tab[:], in0=sc[:].unsqueeze(2).to_broadcast([P, W4, 2]),
+            in1=sign2[:].unsqueeze(1).to_broadcast([P, W4, 2]), op=ALU.mult,
+        )
+        cos_flat = cos_tab[:].rearrange("p j e -> p (j e)")
+
+        def mx_pass(acc, nb, mt, g, c0, c1):
+            s = nb % RING
+            nc.tensor.matmul_mx(
+                out=acc,
+                lhsT=x_codes[:, g, mt * 256 : (mt + 1) * 256].bitcast(FP4X4),
+                lhsT_scale=x_planes[:, g, mt * P : (mt + 1) * P],
+                rhs=w_codes[s][:, g, 2 * c0 : 2 * c1].bitcast(FP4X4),
+                rhs_scale=w_planes[s][:, g, c0:c1],
+                start=(g == 0),
+                stop=(g == PASSES - 1),
+            )
+
+        def rotate_and_store(acc, nb, mt, c0, width, add_engine):
+            heads = max(1, width // HEAD)
+            span = width // heads
+            d0 = c0 % HEAD
+            t0 = mt * HEAD + d0
+            p1 = work.tile([P, BLOCK], F32, name="p1", tag="p1")
+            p2 = work.tile([P, BLOCK], F32, name="p2", tag="p2")
+            o = outs.tile([P, BLOCK], F32, name="o", tag="o")
+            ct = cos_flat[:, t0 : t0 + span].unsqueeze(1).to_broadcast([P, heads, span])
+            st = sin_tab[:, t0 // 2 : (t0 + span) // 2, :].unsqueeze(1).to_broadcast([P, heads, span // 2, 2])
+            nc.vector.tensor_tensor(
+                out=p1[:, 0:width].rearrange("p (h d) -> p h d", h=heads),
+                in0=acc.rearrange("p (h d) -> p h d", h=heads), in1=ct, op=ALU.mult,
+            )
+            nc.vector.tensor_tensor(
+                out=p2[:, 0:width].rearrange("p (h j e) -> p h j e", h=heads, e=2),
+                in0=acc.rearrange("p (h j e) -> p h j e", h=heads, e=2)[:, :, :, ::-1], in1=st, op=ALU.mult,
+            )
+            add_engine.tensor_tensor(out=o[:, 0:width], in0=p1[:, 0:width], in1=p2[:, 0:width], op=ALU.add)
+            head0 = (nb * BLOCK + c0) // HEAD
+            dst = out_0 if head0 < 16 else out_1
+            h = head0 % 16
+            nc.scalar.dma_start(
+                out=dst[h : h + heads, mt * P : (mt + 1) * P, d0 : d0 + span].rearrange("h t d -> t h d"),
+                in_=o[:, 0:width].rearrange("p (h d) -> p h d", h=heads),
+            )
+
+        accs = []
+        for mt in range(TOK_TILES):
+            acc = psum.tile([P, BLOCK], F32, name="acc", tag="acc")
+            accs.append(acc)
+        for g in range(PASSES):
+            for mt in range(TOK_TILES):
+                mx_pass(accs[mt][:], 0, mt, g, 0, BLOCK)
+        load_block(RING)
+        for mt in range(TOK_TILES):
+            rotate_and_store(accs[mt][:], 0, mt, 0, BLOCK, nc.gpsimd)
+
+        for nb in range(1, BLOCKS):
+            for mt in range(TOK_TILES):
+                widths = [BLOCK]
+                if nb == BLOCKS - 1:
+                    widths = LAST_WIDTHS[mt]
+                c0 = 0
+                for width in widths:
+                    last = nb == BLOCKS - 1 and mt == TOK_TILES - 1 and c0 + width == BLOCK
+                    acc = psum.tile([P, BLOCK], F32, name="acc", tag="acc")
+                    for g in range(PASSES):
+                        mx_pass(acc[:, 0:width], nb, mt, g, c0, c0 + width)
+                    rotate_and_store(acc[:, 0:width], nb, mt, c0, width, nc.vector if last else nc.gpsimd)
+                    c0 += width
+            if nb + RING < BLOCKS:
+                load_block(nb + RING)

@@ -19,7 +19,8 @@ BLOCKS = 16
 HEAD = 256
 PAIRS = 128
 RING = 6
-WARM = 18
+WARM = 12
+HEAD_PASSES = 4
 LAST_WIDTHS = [[512], [512], [256, 256], [256, 128, 128]]
 
 FLOPS = 2 * 512 * 4096 * 8192
@@ -54,11 +55,11 @@ def tile_attentionblock_pa_kernel(tc, x_words, x_scales, W_qk_words, W_qk_scales
                 in_=words[g0:g1, :, c0:c1].rearrange("g p n -> p g n").bitcast(I32),
             )
 
-        def load_scales(dst, scales, c0, c1):
+        def load_scales(dst, scales, c0, c1, g0=0, g1=PASSES):
             for q in range(4):
                 nc.sync.dma_start(
-                    out=dst[32 * q : 32 * q + 4, :, :].bitcast(I32),
-                    in_=scales[:, 4 * q : 4 * q + 4, c0:c1].rearrange("g r n -> r g n").bitcast(I32),
+                    out=dst[32 * q : 32 * q + 4, g0:g1, :].bitcast(I32),
+                    in_=scales[g0:g1, 4 * q : 4 * q + 4, c0:c1].rearrange("g r n -> r g n").bitcast(I32),
                 )
 
         def load_block(nb):
@@ -71,8 +72,11 @@ def tile_attentionblock_pa_kernel(tc, x_words, x_scales, W_qk_words, W_qk_scales
         warm_acc = psum.tile([P, BLOCK], F32, name="acc", tag="acc")
         for i in range(WARM):
             nc.tensor.matmul(out=warm_acc[:], lhsT=warm_src[:, 0:P], rhs=warm_src[:], start=True, stop=True)
-        nc.gpsimd.memset(x_planes[:].bitcast(F32), 0.0)
-        nc.vector.memset(w_planes[0][:].bitcast(I32), 0)
+        H = HEAD_PASSES
+        nc.gpsimd.memset(x_planes[:, 0:H, :].bitcast(F32), 0.0)
+        nc.vector.memset(w_planes[0][:, 0:H, :].bitcast(I32), 0)
+        nc.gpsimd.memset(x_planes[:, H:PASSES, :].bitcast(F32), 0.0)
+        nc.vector.memset(w_planes[0][:, H:PASSES, :].bitcast(I32), 0)
 
         pos_i = keep.tile([P, TOK_TILES], I32, name="pos_i")
         nc.gpsimd.iota(pos_i[:], pattern=[[P, TOK_TILES]], base=0, channel_multiplier=1)
@@ -81,14 +85,16 @@ def tile_attentionblock_pa_kernel(tc, x_words, x_scales, W_qk_words, W_qk_scales
         for s in range(1, RING):
             nc.gpsimd.memset(w_planes[s][:].bitcast(F32), 0.0)
 
-        load_codes(x_codes, x_words, 0, 2, 0, 1024)
-        load_codes(w_codes[0], W_qk_words, 0, 2, 0, 1024)
-        load_scales(x_planes, x_scales, 0, 512)
-        load_scales(w_planes[0], W_qk_scales, 0, BLOCK)
-        load_codes(x_codes, x_words, 2, 5, 0, 1024)
-        load_codes(w_codes[0], W_qk_words, 2, 5, 0, 1024)
-        load_codes(x_codes, x_words, 5, 8, 0, 1024)
-        load_codes(w_codes[0], W_qk_words, 5, 8, 0, 1024)
+        load_codes(x_codes, x_words, 0, 1, 0, 1024)
+        load_codes(w_codes[0], W_qk_words, 0, 1, 0, 1024)
+        load_scales(x_planes, x_scales, 0, 512, 0, H)
+        load_scales(w_planes[0], W_qk_scales, 0, BLOCK, 0, H)
+        load_codes(x_codes, x_words, 1, H, 0, 1024)
+        load_codes(w_codes[0], W_qk_words, 1, H, 0, 1024)
+        load_scales(x_planes, x_scales, 0, 512, H, PASSES)
+        load_codes(x_codes, x_words, H, PASSES, 0, 1024)
+        load_codes(w_codes[0], W_qk_words, H, PASSES, 0, 1024)
+        load_scales(w_planes[0], W_qk_scales, 0, BLOCK, H, PASSES)
         for nb in range(1, RING):
             load_block(nb)
 

@@ -20,6 +20,8 @@ HEAD = 256
 PAIRS = 128
 RING = 6
 WARM = 12
+X_PLANE_SHIFT = 64
+W_PLANE_SHIFT = 128
 HEAD_PASSES = 4
 LAST_WIDTHS = [[512], [512], [256, 256], [256, 128, 128]]
 
@@ -39,15 +41,18 @@ def tile_attentionblock_pa_kernel(tc, x_words, x_scales, W_qk_words, W_qk_scales
         psum = ctx.enter_context(tc.psum_pool(name="psum", bufs=8))
         ctx.enter_context(tc.manual_schedule())
 
-        x_codes = keep.tile([P, PASSES, 2 * 512], U8, name="x_codes", align_bytes=64)
-        x_planes = keep.tile([P, PASSES, 512], U8, name="x_planes", align_bytes=64)
+        x_codes = keep.tile([P, PASSES, 2 * 512], U8, name="x_codes", align_bytes=256)
+        x_planes_t = keep.tile([P, 256 + PASSES * 512], U8, name="x_planes_t", align_bytes=256)
+        x_planes = x_planes_t[:, X_PLANE_SHIFT : X_PLANE_SHIFT + PASSES * 512].rearrange("p (g n) -> p g n", g=PASSES)
         w_codes = []
         w_planes = []
         for s in range(RING):
-            wc = keep.tile([P, PASSES, 2 * BLOCK], U8, name="w_codes%d" % s, align_bytes=64)
-            wp = keep.tile([P, PASSES, BLOCK], U8, name="w_planes%d" % s, align_bytes=64)
+            wc = keep.tile([P, PASSES, 2 * BLOCK], U8, name="w_codes%d" % s, align_bytes=256)
+            wp = keep.tile([P, 256 + PASSES * BLOCK], U8, name="w_planes%d" % s, align_bytes=256)
             w_codes.append(wc)
-            w_planes.append(wp)
+            w_planes.append(
+                wp[:, W_PLANE_SHIFT : W_PLANE_SHIFT + PASSES * BLOCK].rearrange("p (g n) -> p g n", g=PASSES)
+            )
 
         def load_codes(dst, words, g0, g1, c0, c1):
             nc.sync.dma_start(
@@ -83,7 +88,7 @@ def tile_attentionblock_pa_kernel(tc, x_words, x_scales, W_qk_words, W_qk_scales
         zero1 = keep.tile([P, 1], F32, name="zero1")
         nc.gpsimd.memset(zero1[:], 0.0)
         for s in range(1, RING):
-            nc.gpsimd.memset(w_planes[s][:].bitcast(F32), 0.0)
+            nc.gpsimd.memset(w_planes[s][:, :, :].bitcast(F32), 0.0)
 
         load_codes(x_codes, x_words, 0, 1, 0, 1024)
         load_codes(w_codes[0], W_qk_words, 0, 1, 0, 1024)

@@ -207,6 +207,40 @@ def tile_attentionblock_pa_kernel(tc, x_words, x_scales, W_qk_words, W_qk_scales
                 in_=o[:, 0:width].rearrange("p (h d) -> p h d", h=heads),
             )
 
+        pending = []
+
+        def finish_pending():
+            for (p1, p2, nb, mt) in pending:
+                o = outs.tile([P, BLOCK], F32, name="o", tag="o")
+                nc.vector.tensor_tensor(out=o[:], in0=p1[:], in1=p2[:], op=ALU.add)
+                head0 = nb * BLOCK // HEAD
+                dst = out_0 if head0 < 16 else out_1
+                h = head0 % 16
+                nc.sync.dma_start(
+                    out=dst[h : h + 2, mt * P : (mt + 1) * P, :].rearrange("h t d -> t h d"),
+                    in_=o[:].rearrange("p (h d) -> p h d", h=2),
+                )
+            pending.clear()
+
+        def rotate_from_copy(acc, nb, mt):
+            t0 = mt * HEAD
+            y = work.tile([P, BLOCK], F32, name="y", tag="y")
+            p1 = work.tile([P, BLOCK], F32, name="p1", tag="p1")
+            p2 = work.tile([P, BLOCK], F32, name="p2", tag="p2")
+            nc.scalar.copy(out=y[:], in_=acc)
+            ct = cos_flat[:, t0 : t0 + HEAD].unsqueeze(1).to_broadcast([P, 2, HEAD])
+            st = sin_tab[:, t0 // 2 : (t0 + HEAD) // 2, :].unsqueeze(1).to_broadcast([P, 2, PAIRS, 2])
+            nc.vector.tensor_tensor(
+                out=p1[:].rearrange("p (h d) -> p h d", h=2), in0=y[:].rearrange("p (h d) -> p h d", h=2), in1=ct,
+                op=ALU.mult,
+            )
+            nc.vector.tensor_tensor(
+                out=p2[:].rearrange("p (h j e) -> p h j e", h=2, e=2),
+                in0=y[:].rearrange("p (h j e) -> p h j e", h=2, e=2)[:, :, :, ::-1], in1=st, op=ALU.mult,
+            )
+            finish_pending()
+            pending.append((p1, p2, nb, mt))
+
         accs = []
         for mt in range(TOK_TILES):
             acc = psum.tile([P, BLOCK], F32, name="acc", tag="acc")
@@ -216,7 +250,7 @@ def tile_attentionblock_pa_kernel(tc, x_words, x_scales, W_qk_words, W_qk_scales
                 mx_pass(accs[mt][:], 0, mt, g, 0, BLOCK)
         load_block(RING)
         for mt in range(TOK_TILES):
-            rotate_and_store(accs[mt][:], 0, mt, 0, BLOCK, nc.gpsimd)
+            rotate_from_copy(accs[mt][:], 0, mt)
 
         for nb in range(1, BLOCKS):
             for mt in range(TOK_TILES):
@@ -229,7 +263,11 @@ def tile_attentionblock_pa_kernel(tc, x_words, x_scales, W_qk_words, W_qk_scales
                     acc = psum.tile([P, BLOCK], F32, name="acc", tag="acc")
                     for g in range(PASSES):
                         mx_pass(acc[:, 0:width], nb, mt, g, c0, c0 + width)
-                    rotate_and_store(acc[:, 0:width], nb, mt, c0, width, nc.vector if last else nc.gpsimd)
+                    if nb == BLOCKS - 1:
+                        finish_pending()
+                        rotate_and_store(acc[:, 0:width], nb, mt, c0, width, nc.vector if last else nc.gpsimd)
+                    else:
+                        rotate_from_copy(acc[:, 0:width], nb, mt)
                     c0 += width
             if nb + RING < BLOCKS:
                 load_block(nb + RING)

@@ -61,7 +61,7 @@ def tile_attentionblock_pa_kernel(tc, x_words, x_scales, W_qk_words, W_qk_scales
             )
 
         def load_scales(dst, scales, c0, c1, g0=0, g1=PASSES):
-            for q in range(4):
+            for q in (0, 2, 1, 3):
                 nc.sync.dma_start(
                     out=dst[32 * q : 32 * q + 4, g0:g1, :].bitcast(I32),
                     in_=scales[g0:g1, 4 * q : 4 * q + 4, c0:c1].rearrange("g r n -> r g n").bitcast(I32),

@@ -20,6 +20,7 @@ HEAD = 256
 PAIRS = 128
 RING = 6
 WARM = 12
+X_CODE_SHIFT = 128
 X_PLANE_SHIFT = 64
 W_PLANE_SHIFT = 128
 HEAD_PASSES = 4
@@ -41,7 +42,8 @@ def tile_attentionblock_pa_kernel(tc, x_words, x_scales, W_qk_words, W_qk_scales
         psum = ctx.enter_context(tc.psum_pool(name="psum", bufs=8))
         ctx.enter_context(tc.manual_schedule())
 
-        x_codes = keep.tile([P, PASSES, 2 * 512], U8, name="x_codes", align_bytes=256)
+        x_codes_t = keep.tile([P, 256 + PASSES * 1024], U8, name="x_codes_t", align_bytes=256)
+        x_codes = x_codes_t[:, X_CODE_SHIFT : X_CODE_SHIFT + PASSES * 1024].rearrange("p (g n) -> p g n", g=PASSES)
         x_planes_t = keep.tile([P, 256 + PASSES * 512], U8, name="x_planes_t", align_bytes=256)
         x_planes = x_planes_t[:, X_PLANE_SHIFT : X_PLANE_SHIFT + PASSES * 512].rearrange("p (g n) -> p g n", g=PASSES)
         w_codes = []

@@ -204,7 +204,7 @@ def tile_attentionblock_pa_kernel(tc, x_words, x_scales, W_qk_words, W_qk_scales
             head0 = (nb * BLOCK + c0) // HEAD
             dst = out_0 if head0 < 16 else out_1
             h = head0 % 16
-            nc.scalar.dma_start(
+            nc.sync.dma_start(
                 out=dst[h : h + heads, mt * P : (mt + 1) * P, d0 : d0 + span].rearrange("h t d -> t h d"),
                 in_=o[:, 0:width].rearrange("p (h d) -> p h d", h=heads),
             )

from contextlib import ExitStack
import math

import concourse.mybir as mybir

F32 = mybir.dt.float32
BF16 = mybir.dt.bfloat16
I32 = mybir.dt.int32
U8 = mybir.dt.uint8
FP4X4 = mybir.dt.float4_e2m1fn_x4
ALU = mybir.AluOpType
ACT = mybir.ActivationFunctionType

P = 128
PASSES = 8
TOK_TILES = 4
BLOCK = 512
BLOCKS = 16
HEAD = 256
PAIRS = 128
RING = 6
WARM = 12
X_CODE_SHIFT = 128
X_PLANE_SHIFT = 64
W_PLANE_SHIFT = 128
HEAD_PASSES = 4
LAST_WIDTHS = [[512], [512], [256, 256], [256, 128, 128]]

FLOPS = 2 * 512 * 4096 * 8192

TWO_PI = 2.0 * math.pi
TWO_PI_HI = 6.28125
TWO_PI_LO = TWO_PI - TWO_PI_HI


def tile_attentionblock_pa_kernel(tc, x_words, x_scales, W_qk_words, W_qk_scales, out_0, out_1):
    nc = tc.nc
    with ExitStack() as ctx:
        keep = ctx.enter_context(tc.tile_pool(name="keep", bufs=1))
        work = ctx.enter_context(tc.tile_pool(name="work", bufs=6))
        outs = ctx.enter_context(tc.tile_pool(name="outs", bufs=8))
        psum = ctx.enter_context(tc.psum_pool(name="psum", bufs=8))
        ctx.enter_context(tc.manual_schedule())

        x_codes_t = keep.tile([P, 256 + PASSES * 1024], U8, name="x_codes_t", align_bytes=256)
        x_codes = x_codes_t[:, X_CODE_SHIFT : X_CODE_SHIFT + PASSES * 1024].rearrange("p (g n) -> p g n", g=PASSES)
        x_planes_t = keep.tile([P, 256 + PASSES * 512], U8, name="x_planes_t", align_bytes=256)
        x_planes = x_planes_t[:, X_PLANE_SHIFT : X_PLANE_SHIFT + PASSES * 512].rearrange("p (g n) -> p g n", g=PASSES)
        w_codes = []
        w_planes = []
        for s in range(RING):
            wc = keep.tile([P, PASSES, 2 * BLOCK], U8, name="w_codes%d" % s, align_bytes=256)
            wp = keep.tile([P, 256 + PASSES * BLOCK], U8, name="w_planes%d" % s, align_bytes=256)
            w_codes.append(wc)
            w_planes.append(
                wp[:, W_PLANE_SHIFT : W_PLANE_SHIFT + PASSES * BLOCK].rearrange("p (g n) -> p g n", g=PASSES)
            )

        def load_codes(dst, words, g0, g1, c0, c1):
            nc.sync.dma_start(
                out=dst[:, g0:g1, :].bitcast(I32),
                in_=words[g0:g1, :, c0:c1].rearrange("g p n -> p g n").bitcast(I32),
            )

        def load_scales(dst, scales, c0, c1, g0=0, g1=PASSES):
            for q in (0, 2, 1, 3):
                nc.sync.dma_start(
                    out=dst[32 * q : 32 * q + 4, g0:g1, :].bitcast(I32),
                    in_=scales[g0:g1, 4 * q : 4 * q + 4, c0:c1].rearrange("g r n -> r g n").bitcast(I32),
                )

        def load_block(nb):
            s = nb % RING
            load_scales(w_planes[s], W_qk_scales, nb * BLOCK, (nb + 1) * BLOCK)
            load_codes(w_codes[s], W_qk_words, 0, PASSES, nb * 2 * BLOCK, (nb + 1) * 2 * BLOCK)

        warm_src = keep.tile([P, BLOCK], BF16, name="warm_src")
        nc.vector.memset(warm_src[:], 1.0)
        warm_acc = psum.tile([P, BLOCK], F32, name="acc", tag="acc")
        for i in range(WARM):
            nc.tensor.matmul(out=warm_acc[:], lhsT=warm_src[:, 0:P], rhs=warm_src[:], start=True, stop=True)
        H = HEAD_PASSES
        nc.gpsimd.memset(x_planes[:, 0:H, :].bitcast(F32), 0.0)
        nc.vector.memset(w_planes[0][:, 0:H, :].bitcast(I32), 0)
        nc.gpsimd.memset(x_planes[:, H:PASSES, :].bitcast(F32), 0.0)
        nc.vector.memset(w_planes[0][:, H:PASSES, :].bitcast(I32), 0)

        pos_i = keep.tile([P, TOK_TILES], I32, name="pos_i")
        nc.gpsimd.iota(pos_i[:], pattern=[[P, TOK_TILES]], base=0, channel_multiplier=1)
        zero1 = keep.tile([P, 1], F32, name="zero1")
        nc.gpsimd.memset(zero1[:], 0.0)
        for s in range(1, RING):
            nc.gpsimd.memset(w_planes[s][:, :, :].bitcast(F32), 0.0)

        load_codes(x_codes, x_words, 0, 1, 0, 1024)
        load_codes(w_codes[0], W_qk_words, 0, 1, 0, 1024)
        load_scales(x_planes, x_scales, 0, 512, 0, H)
        load_scales(w_planes[0], W_qk_scales, 0, BLOCK, 0, H)
        load_codes(x_codes, x_words, 1, H, 0, 1024)
        load_codes(w_codes[0], W_qk_words, 1, H, 0, 1024)
        load_scales(x_planes, x_scales, 0, 512, H, PASSES)
        load_codes(x_codes, x_words, H, PASSES, 0, 1024)
        load_codes(w_codes[0], W_qk_words, H, PASSES, 0, 1024)
        load_scales(w_planes[0], W_qk_scales, 0, BLOCK, H, PASSES)
        for nb in range(1, RING):
            load_block(nb)

        warm = keep.tile([P, 1], F32, name="warm")
        nc.scalar.activation(out=warm[:], in_=zero1[:], func=ACT.Sin)

        W4 = TOK_TILES * PAIRS
        pos_f = keep.tile([P, TOK_TILES], F32, name="pos_f")
        nc.vector.tensor_copy(out=pos_f[:], in_=pos_i[:])
        freq = keep.tile([P, PAIRS], F32, name="freq")
        nc.vector.memset(freq[:, 0:1], 1.0)
        for b in range(7):
            w = 1 << b
            nc.vector.tensor_scalar(
                out=freq[:, w : 2 * w], in0=freq[:, 0:w], scalar1=10000.0 ** (-w / 128.0), scalar2=None, op0=ALU.mult
            )
        ang = keep.tile([P, W4], F32, name="ang")
        for mt in range(TOK_TILES):
            nc.vector.tensor_scalar(
                out=ang[:, mt * PAIRS : (mt + 1) * PAIRS], in0=freq[:], scalar1=pos_f[:, mt : mt + 1], scalar2=None,
                op0=ALU.mult,
            )
        turns_i = keep.tile([P, W4], I32, name="turns_i")
        nc.vector.tensor_scalar(
            out=turns_i[:], in0=ang[:], scalar1=1.0 / TWO_PI, scalar2=0.25, op0=ALU.mult, op1=ALU.add
        )
        turns = keep.tile([P, W4], F32, name="turns")
        nc.vector.tensor_copy(out=turns[:], in_=turns_i[:])
        red_hi = keep.tile([P, W4], F32, name="red_hi")
        nc.vector.scalar_tensor_tensor(
            out=red_hi[:], in0=turns[:], scalar=-TWO_PI_HI, in1=ang[:], op0=ALU.mult, op1=ALU.add
        )
        red = keep.tile([P, W4], F32, name="red")
        nc.vector.scalar_tensor_tensor(
            out=red[:], in0=turns[:], scalar=-TWO_PI_LO, in1=red_hi[:], op0=ALU.mult, op1=ALU.add
        )
        sin_half = keep.tile([P, W4], F32, name="sin_half")
        nc.scalar.activation(out=sin_half[:], in_=red[:], func=ACT.Sin, scale=0.5)
        neg_abs = keep.tile([P, W4], F32, name="neg_abs")
        nc.vector.scalar_tensor_tensor(
            out=neg_abs[:], in0=red[:], scalar=-1.0, in1=red[:], op0=ALU.mult, op1=ALU.min
        )
        co_arg = keep.tile([P, W4], F32, name="co_arg")
        nc.vector.tensor_scalar(
            out=co_arg[:], in0=neg_abs[:], scalar1=0.5, scalar2=0.5 * math.pi, op0=ALU.mult, op1=ALU.add
        )
        cos_half = keep.tile([P, W4], F32, name="cos_half")
        nc.scalar.activation(out=cos_half[:], in_=co_arg[:], func=ACT.Sin)

        sq = keep.tile([P, W4], F32, name="sq")
        nc.vector.tensor_tensor(out=sq[:], in0=sin_half[:], in1=sin_half[:], op=ALU.mult)
        cos_tab = keep.tile([P, W4, 2], F32, name="cos_tab")
        nc.vector.tensor_scalar(
            out=cos_tab[:], in0=sq[:].unsqueeze(2).to_broadcast([P, W4, 2]), scalar1=-2.0, scalar2=1.0,
            op0=ALU.mult, op1=ALU.add,
        )
        sign2 = keep.tile([P, 2], F32, name="sign2")
        nc.vector.memset(sign2[:, 0:1], -2.0)
        nc.vector.memset(sign2[:, 1:2], 2.0)
        sc = keep.tile([P, W4], F32, name="sc")
        nc.vector.tensor_tensor(out=sc[:], in0=sin_half[:], in1=cos_half[:], op=ALU.mult)
        sin_tab = keep.tile([P, W4, 2], F32, name="sin_tab")
        nc.vector.tensor_tensor(
            out=sin_tab[:], in0=sc[:].unsqueeze(2).to_broadcast([P, W4, 2]),
            in1=sign2[:].unsqueeze(1).to_broadcast([P, W4, 2]), op=ALU.mult,
        )
        cos_flat = cos_tab[:].rearrange("p j e -> p (j e)")

        def mx_pass(acc, nb, mt, g, c0, c1):
            s = nb % RING
            nc.tensor.matmul_mx(
                out=acc,
                lhsT=x_codes[:, g, mt * 256 : (mt + 1) * 256].bitcast(FP4X4),
                lhsT_scale=x_planes[:, g, mt * P : (mt + 1) * P],
                rhs=w_codes[s][:, g, 2 * c0 : 2 * c1].bitcast(FP4X4),
                rhs_scale=w_planes[s][:, g, c0:c1],
                start=(g == 0),
                stop=(g == PASSES - 1),
            )

        def rotate_and_store(acc, nb, mt, c0, width, add_engine):
            heads = max(1, width // HEAD)
            span = width // heads
            d0 = c0 % HEAD
            t0 = mt * HEAD + d0
            p1 = work.tile([P, BLOCK], F32, name="p1", tag="p1")
            p2 = work.tile([P, BLOCK], F32, name="p2", tag="p2")
            o = outs.tile([P, BLOCK], F32, name="o", tag="o")
            ct = cos_flat[:, t0 : t0 + span].unsqueeze(1).to_broadcast([P, heads, span])
            st = sin_tab[:, t0 // 2 : (t0 + span) // 2, :].unsqueeze(1).to_broadcast([P, heads, span // 2, 2])
            nc.vector.tensor_tensor(
                out=p1[:, 0:width].rearrange("p (h d) -> p h d", h=heads),
                in0=acc.rearrange("p (h d) -> p h d", h=heads), in1=ct, op=ALU.mult,
            )
            nc.vector.tensor_tensor(
                out=p2[:, 0:width].rearrange("p (h j e) -> p h j e", h=heads, e=2),
                in0=acc.rearrange("p (h j e) -> p h j e", h=heads, e=2)[:, :, :, ::-1], in1=st, op=ALU.mult,
            )
            add_engine.tensor_tensor(out=o[:, 0:width], in0=p1[:, 0:width], in1=p2[:, 0:width], op=ALU.add)
            head0 = (nb * BLOCK + c0) // HEAD
            dst = out_0 if head0 < 16 else out_1
            h = head0 % 16
            nc.sync.dma_start(
                out=dst[h : h + heads, mt * P : (mt + 1) * P, d0 : d0 + span].rearrange("h t d -> t h d"),
                in_=o[:, 0:width].rearrange("p (h d) -> p h d", h=heads),
            )

        pending = []

        def finish_pending():
            for (p1, p2, nb, mt) in pending:
                o = outs.tile([P, BLOCK], F32, name="o", tag="o")
                nc.vector.tensor_tensor(out=o[:], in0=p1[:], in1=p2[:], op=ALU.add)
                head0 = nb * BLOCK // HEAD
                dst = out_0 if head0 < 16 else out_1
                h = head0 % 16
                nc.sync.dma_start(
                    out=dst[h : h + 2, mt * P : (mt + 1) * P, :].rearrange("h t d -> t h d"),
                    in_=o[:].rearrange("p (h d) -> p h d", h=2),
                )
            pending.clear()

        def rotate_from_copy(acc, nb, mt):
            t0 = mt * HEAD
            y = work.tile([P, BLOCK], F32, name="y", tag="y")
            p1 = work.tile([P, BLOCK], F32, name="p1", tag="p1")
            p2 = work.tile([P, BLOCK], F32, name="p2", tag="p2")
            nc.scalar.copy(out=y[:], in_=acc)
            ct = cos_flat[:, t0 : t0 + HEAD].unsqueeze(1).to_broadcast([P, 2, HEAD])
            st = sin_tab[:, t0 // 2 : (t0 + HEAD) // 2, :].unsqueeze(1).to_broadcast([P, 2, PAIRS, 2])
            nc.vector.tensor_tensor(
                out=p1[:].rearrange("p (h d) -> p h d", h=2), in0=y[:].rearrange("p (h d) -> p h d", h=2), in1=ct,
                op=ALU.mult,
            )
            nc.vector.tensor_tensor(
                out=p2[:].rearrange("p (h j e) -> p h j e", h=2, e=2),
                in0=y[:].rearrange("p (h j e) -> p h j e", h=2, e=2)[:, :, :, ::-1], in1=st, op=ALU.mult,
            )
            finish_pending()
            pending.append((p1, p2, nb, mt))

        accs = []
        for mt in range(TOK_TILES):
            acc = psum.tile([P, BLOCK], F32, name="acc", tag="acc")
            accs.append(acc)
        for g in range(PASSES):
            for mt in range(TOK_TILES):
                mx_pass(accs[mt][:], 0, mt, g, 0, BLOCK)
        load_block(RING)
        for mt in range(TOK_TILES):
            rotate_from_copy(accs[mt][:], 0, mt)

        for nb in range(1, BLOCKS):
            for mt in range(TOK_TILES):
                widths = [BLOCK]
                if nb == BLOCKS - 1:
                    widths = LAST_WIDTHS[mt]
                c0 = 0
                for width in widths:
                    last = nb == BLOCKS - 1 and mt == TOK_TILES - 1 and c0 + width == BLOCK
                    acc = psum.tile([P, BLOCK], F32, name="acc", tag="acc")
                    for g in range(PASSES):
                        mx_pass(acc[:, 0:width], nb, mt, g, c0, c0 + width)
                    if nb == BLOCKS - 1:
                        finish_pending()
                        rotate_and_store(acc[:, 0:width], nb, mt, c0, width, nc.vector if last else nc.gpsimd)
                    else:
                        rotate_from_copy(acc[:, 0:width], nb, mt)
                    c0 += width
            if nb + RING < BLOCKS:
                load_block(nb + RING)
